import numpy as np
import ml_dtypes


def mxq(x, axis, fmt="e4m3"):
    dtype, down = {"e4m3": (ml_dtypes.float8_e4m3fn, 7), "e5m2": (ml_dtypes.float8_e5m2, 14)}[fmt]
    v = np.moveaxis(np.asarray(x, np.float32).astype(ml_dtypes.bfloat16).astype(np.float64), axis, -1)
    blocks = v.reshape(v.shape[:-1] + (-1, 32))
    amax = np.abs(blocks).max(-1, keepdims=True)
    byte = np.maximum(np.where(amax > 0, np.frexp(amax)[1] - 1 + 127, 0) - down, 1)
    scale = np.exp2(byte - 127.0)
    codes = (blocks / scale).astype(np.float32).astype(dtype).astype(np.float64)
    return np.moveaxis((codes * scale).reshape(v.shape), -1, axis)


WIDE = False


def mx_kscale(k):
    if not WIDE:
        return np.ones(k)
    levels = np.array([10, -10, 5, -5, 0])
    a = np.random.permutation(np.resize(levels, k // 512 * 4)).reshape(k // 512, 4)
    idx = np.arange(k)
    return np.exp2(a[idx // 512, idx % 128 // 32])


BF16 = ml_dtypes.bfloat16


def bf(x):
    return np.asarray(x, np.float32).astype(BF16)


def f64(x):
    return np.asarray(x).astype(np.float64)


N, D, Q, CLIP, R = 4096, 1024, 128, 8, 16
MIX = 0.7
GAIN = 2.0


def unit(v):
    return v / np.sqrt((v * v).sum(-1, keepdims=True))


def setup_inputs():
    s = mx_kscale(D)
    base = np.random.standard_normal((N, D))
    return {"te": bf(unit(np.random.standard_normal((Q, D))) / s),
            "fe_n": bf(unit(base) * s),
            "loc_n": bf(unit(MIX * base + MIX * np.random.standard_normal((N, D))) * s),
            "glob_n": bf(unit(MIX * base + MIX * np.random.standard_normal((N, D))) * s),
            "logit_scale": bf(np.log(GAIN * np.sqrt(D)) + 0.1 * np.random.standard_normal(1)),
            "logit_bias": bf(-1.0 + 0.2 * np.random.standard_normal(1))}


def reference(te, fe_n, loc_n, glob_n, logit_scale, logit_bias):
    tq = mxq(f64(te), 1, "e4m3")
    ls = np.exp(f64(logit_scale))
    b = f64(logit_bias)
    ori = (tq @ mxq(f64(fe_n), 1, "e4m3").T) * ls + b
    loc = (tq @ mxq(f64(loc_n), 1, "e4m3").T) * ls + b
    glo = (tq @ mxq(f64(glob_n), 1, "e4m3").T) * ls + b
    fused = 0.9 * ori + 0.05 * loc + 0.05 * glo
    logits = fused.max(0, keepdims=True)
    x = logits.reshape(logits.shape[0], N // CLIP, CLIP)
    e = np.exp(x - x.max(-1, keepdims=True))
    w = e / e.sum(-1, keepdims=True)
    return (w * x).sum(-1)

@@ -1,0 +1,269 @@
+from contextlib import ExitStack
+
+import concourse.mybir as mybir
+from concourse.masks import make_identity
+
+F32 = mybir.dt.float32
+BF16 = mybir.dt.bfloat16
+U32 = mybir.dt.uint32
+U8 = mybir.dt.uint8
+FP8X4 = mybir.dt.float8_e4m3fn_x4
+ALU = mybir.AluOpType
+ACT = mybir.ActivationFunctionType
+AXIS = mybir.AxisListType
+
+P = 128
+FRAMES = 4096
+FEATURES = 1024
+QUERIES = 128
+CLIP = 8
+MAIN_WEIGHT = 0.9
+SIDE_WEIGHT = 0.05
+
+FLOPS = 2 * 3 * QUERIES * FRAMES * FEATURES
+
+TILES = FRAMES // P
+CLIPS_PER_PARTITION = TILES // CLIP
+K_PASS = 4 * P
+PASSES = FEATURES // K_PASS
+WORDS = FEATURES // 2
+WORD_BLOCKS = WORDS // P
+HALVES = WORD_BLOCKS // PASSES
+BLOCK_TILES = 4
+BLOCKS = TILES // BLOCK_TILES
+
+FE, LOC, GLOB = 0, 1, 2
+
+RUN = 6
+PAIR = 2
+VECTOR_EVERY = 6
+AHEAD = 3
+FOLD = 4
+OUT_ROWS = P // FOLD
+
+
+def work_list():
+    tiles = []
+    for block in range(BLOCKS):
+        for j in range(BLOCK_TILES):
+            tiles.append((LOC, block, j))
+            tiles.append((GLOB, block, j))
+        for j in range(BLOCK_TILES):
+            tiles.append((FE, block, j))
+    return tiles
+
+
+def tile_custommodel_pb_t_kernel(tc, te, fe_n, loc_n, glob_n, logit_scale, logit_bias, out):
+    nc = tc.nc
+    streams = {
+        FE: fe_n.rearrange("(p t) d -> p t d", t=TILES),
+        LOC: loc_n.rearrange("(p t) d -> p t d", t=TILES),
+        GLOB: glob_n.rearrange("(p t) d -> p t d", t=TILES),
+    }
+    tiles = work_list()
+    rounds = [tiles[i : i + RUN] for i in range(0, len(tiles), RUN)]
+
+    with ExitStack() as ctx:
+        keep = ctx.enter_context(tc.tile_pool(name="keep", bufs=1))
+        frames = ctx.enter_context(tc.tile_pool(name="frames", bufs=3 * AHEAD))
+        stage = ctx.enter_context(tc.tile_pool(name="stage", bufs=2 * RUN // PAIR))
+        packed = ctx.enter_context(tc.tile_pool(name="packed", bufs=3 * RUN // PAIR))
+        sums = ctx.enter_context(tc.tile_pool(name="sums", bufs=2))
+        banks = ctx.enter_context(tc.psum_pool(name="banks", bufs=RUN))
+        products = ctx.enter_context(tc.psum_pool(name="products", bufs=1))
+        ctx.enter_context(tc.manual_schedule())
+
+        loaded = {}
+
+        def load(stream, block, first, count):
+            if first == 0:
+                x = frames.tile([P, BLOCK_TILES, FEATURES], BF16, name="x")
+                loaded[(stream, block)] = x
+            t0 = block * BLOCK_TILES + first
+            nc.sync.dma_start(
+                out=loaded[(stream, block)][:, first : first + count, :],
+                in_=streams[stream][:, t0 : t0 + count, :],
+            )
+
+        def transpose_words(rows):
+            bank = banks.tile([P, WORD_BLOCKS, P], F32, name="bank")
+            words = rows.bitcast(F32)
+            for w in range(WORD_BLOCKS):
+                nc.tensor.transpose(bank[:, w, :], words[:, w * P : (w + 1) * P], identity[:])
+            return bank
+
+        def regroup(copy, bank, grouped_rows):
+            copy(
+                out=grouped_rows.bitcast(F32).rearrange("p (g r u) -> p g r u", g=PASSES, u=HALVES),
+                in_=bank[:].rearrange("p (g u) r -> p g r u", u=HALVES),
+            )
+
+        te_rows = keep.tile([P, FEATURES], BF16, name="te_rows")
+        nc.sync.dma_start(out=te_rows[:], in_=te)
+        scale_raw = keep.tile([P, 1], BF16, name="scale_raw")
+        nc.scalar.dma_start(out=scale_raw[:], in_=logit_scale.partition_broadcast(P))
+        bias_raw = keep.tile([P, 1], BF16, name="bias_raw")
+        nc.scalar.dma_start(out=bias_raw[:], in_=logit_bias.partition_broadcast(P))
+
+        for first in range(0, BLOCK_TILES, PAIR):
+            load(LOC, 0, first, PAIR)
+            load(GLOB, 0, first, PAIR)
+        load(FE, 0, 0, BLOCK_TILES)
+        for block in range(1, AHEAD):
+            for stream in (LOC, GLOB, FE):
+                load(stream, block, 0, BLOCK_TILES)
+
+        identity = keep.tile([P, P], F32, name="identity")
+        make_identity(nc, identity[:])
+
+        gain = keep.tile([P, 1], F32, name="gain")
+        nc.scalar.activation(out=gain[:], in_=scale_raw[:], func=ACT.Exp)
+
+        owner = keep.tile([P, OUT_ROWS], F32, name="owner")
+        nc.vector.tensor_reduce(
+            out=owner[:], in_=identity[:].rearrange("p (m b) -> p m b", b=FOLD), axis=AXIS.X, op=ALU.add
+        )
+        gather = keep.tile([P, FOLD, OUT_ROWS], F32, name="gather")
+        nc.vector.tensor_copy(out=gather[:], in_=owner[:].unsqueeze(1).to_broadcast([P, FOLD, OUT_ROWS]))
+        place = keep.tile([P, FOLD], F32, name="place")
+        nc.vector.tensor_reduce(
+            out=place[:], in_=identity[:].rearrange("p (m b) -> p b m", b=FOLD), axis=AXIS.X, op=ALU.add
+        )
+
+        te_bank = transpose_words(te_rows[:])
+        te_grouped = keep.tile([P, FEATURES], BF16, name="te_grouped", align_bytes=64)
+        regroup(nc.vector.tensor_copy, te_bank, te_grouped[:])
+        te_codes = keep.tile([P, PASSES * QUERIES], U32, name="te_codes", align_bytes=64)
+        te_scales = keep.tile([P, PASSES * QUERIES], U8, name="te_scales", align_bytes=64)
+        nc.vector.quantize_mx(out=te_codes[:].bitcast(FP8X4), scales=te_scales[:], in_=te_grouped[:])
+        bias = keep.tile([P, 1], F32, name="bias")
+        nc.vector.tensor_copy(out=bias[:], in_=bias_raw[:])
+        main_gain = keep.tile([P, 1], F32, name="main_gain")
+        nc.vector.tensor_scalar_mul(out=main_gain[:], in0=gain[:], scalar1=MAIN_WEIGHT)
+        side_gain = keep.tile([P, 1], F32, name="side_gain")
+        nc.vector.tensor_scalar_mul(out=side_gain[:], in0=gain[:], scalar1=SIDE_WEIGHT)
+
+        logits = keep.tile([P, CLIPS_PER_PARTITION, CLIP], F32, name="logits")
+
+        def transpose_round(step):
+            filled = []
+            for stream, block, j in rounds[step]:
+                filled.append(transpose_words(loaded[(stream, block)][:, j, :]))
+                if j == BLOCK_TILES - 1 and block + AHEAD < BLOCKS:
+                    load(stream, block + AHEAD, 0, BLOCK_TILES)
+            pairs = []
+            for n, bank in enumerate(filled):
+                if n % PAIR == 0:
+                    grouped = stage.tile([P, PAIR * FEATURES], BF16, name="grouped", align_bytes=64)
+                    pairs.append(grouped)
+                copy = nc.vector.tensor_copy if (step * RUN + n) % VECTOR_EVERY == 0 else nc.scalar.copy
+                s = n % PAIR
+                regroup(copy, bank, pairs[-1][:, s * FEATURES : (s + 1) * FEATURES])
+            return pairs
+
+        def quantise_round(pairs):
+            quantised = []
+            for grouped in pairs:
+                codes = packed.tile([P, PAIR * PASSES * P], U32, name="codes", align_bytes=64)
+                scales = packed.tile([P, PAIR * PASSES * P], U8, name="scales", align_bytes=64)
+                nc.vector.quantize_mx(out=codes[:].bitcast(FP8X4), scales=scales[:], in_=grouped[:])
+                quantised.append((codes, scales))
+            return quantised
+
+        current = {}
+
+        def multiply_round(step, quantised):
+            for n, (stream, block, j) in enumerate(rounds[step]):
+                codes, scales = quantised[n // PAIR]
+                if j == 0 and stream == FE:
+                    current["main"] = products.tile([P, BLOCK_TILES * QUERIES], F32, name="main")
+                if j == 0 and stream == LOC:
+                    current["side"] = products.tile([P, BLOCK_TILES * QUERIES], F32, name="side")
+                product = current["main"] if stream == FE else current["side"]
+                for g in range(PASSES):
+                    cols = slice(((n % PAIR) * PASSES + g) * P, ((n % PAIR) * PASSES + g + 1) * P)
+                    te_cols = slice(g * QUERIES, (g + 1) * QUERIES)
+                    nc.tensor.matmul_mx(
+                        out=product[:, j * QUERIES : (j + 1) * QUERIES],
+                        lhsT=codes[:, cols].bitcast(FP8X4),
+                        lhsT_scale=scales[:, cols],
+                        rhs=te_codes[:, te_cols].bitcast(FP8X4),
+                        rhs_scale=te_scales[:, te_cols],
+                        start=(stream != GLOB and g == 0),
+                        stop=(stream != LOC and g == PASSES - 1),
+                    )
+                if j == BLOCK_TILES - 1 and stream == GLOB:
+                    current["weighted"] = sums.tile([P, BLOCK_TILES * QUERIES], F32, name="weighted")
+                    nc.scalar.activation(
+                        out=current["weighted"][:],
+                        in_=product[:],
+                        func=ACT.Identity,
+                        scale=side_gain[:, 0:1],
+                        bias=bias[:, 0:1],
+                    )
+                if j == BLOCK_TILES - 1 and stream == FE:
+                    fused = sums.tile([P, BLOCK_TILES, QUERIES], F32, name="fused")
+                    nc.vector.scalar_tensor_tensor(
+                        out=fused[:].rearrange("p t q -> p (t q)"),
+                        in0=product[:],
+                        scalar=main_gain[:, 0:1],
+                        in1=current["weighted"][:],
+                        op0=ALU.mult,
+                        op1=ALU.add,
+                    )
+                    nc.vector.tensor_reduce(
+                        out=logits[:].rearrange("p c j -> p (c j)")[:, block * BLOCK_TILES : (block + 1) * BLOCK_TILES],
+                        in_=fused[:],
+                        axis=AXIS.X,
+                        op=ALU.max,
+                    )
+
+        grouped_of = {}
+        quantised_of = {}
+        for step in range(len(rounds) + 2):
+            if step < len(rounds):
+                grouped_of[step] = transpose_round(step)
+            if 1 <= step <= len(rounds):
+                quantised_of[step - 1] = quantise_round(grouped_of[step - 1])
+            if step >= 2:
+                multiply_round(step - 2, quantised_of[step - 2])
+
+        shape = [P, CLIPS_PER_PARTITION, CLIP]
+        top = keep.tile([P, CLIPS_PER_PARTITION], F32, name="top")
+        nc.vector.tensor_reduce(out=top[:], in_=logits[:], axis=AXIS.X, op=ALU.max)
+        shifted = keep.tile(shape, F32, name="shifted")
+        nc.vector.tensor_tensor(
+            out=shifted[:], in0=logits[:], in1=top[:].unsqueeze(2).to_broadcast(shape), op=ALU.subtract
+        )
+        terms = keep.tile([P, 2] + shape[1:], F32, name="terms")
+        nc.scalar.activation(out=terms[:, 0], in_=shifted[:], func=ACT.Exp)
+        nc.vector.tensor_tensor(out=terms[:, 1], in0=terms[:, 0], in1=logits[:], op=ALU.mult)
+        totals = keep.tile([P, 2 * CLIPS_PER_PARTITION], F32, name="totals")
+        nc.vector.tensor_reduce(
+            out=totals[:], in_=terms[:].rearrange("p h c j -> p (h c) j"), axis=AXIS.X, op=ALU.add
+        )
+
+        wide = [P, FOLD, 2 * CLIPS_PER_PARTITION]
+        spread = keep.tile(wide, F32, name="spread")
+        nc.vector.tensor_tensor(
+            out=spread[:],
+            in0=totals[:].unsqueeze(1).to_broadcast(wide),
+            in1=place[:].unsqueeze(2).to_broadcast(wide),
+            op=ALU.mult,
+        )
+        folded = banks.tile([P, FOLD, 2, CLIPS_PER_PARTITION], F32, name="folded", tag="bank")
+        nc.tensor.matmul(
+            out=folded[:].rearrange("p b h c -> p (b h c)"),
+            lhsT=gather[:].rearrange("p r m -> p (r m)"),
+            rhs=spread[:].rearrange("p b k -> p (b k)"),
+            start=True,
+            stop=True,
+        )
+        inverse = keep.tile([P, FOLD, CLIPS_PER_PARTITION], F32, name="inverse")
+        nc.vector.reciprocal(out=inverse[:], in_=folded[:, :, 0, :])
+        pooled = keep.tile([P, FOLD, CLIPS_PER_PARTITION], F32, name="pooled")
+        nc.vector.tensor_tensor(out=pooled[:], in0=folded[:, :, 1, :], in1=inverse[:], op=ALU.mult)
+        nc.sync.dma_start(
+            out=out.rearrange("o (m k) -> (o m) k", k=FOLD * CLIPS_PER_PARTITION),
+            in_=pooled[0:OUT_ROWS].rearrange("p b c -> p (b c)"),
+        )

@@ -34,7 +34,9 @@ BLOCKS = TILES // BLOCK_TILES
 
 FE, LOC, GLOB = 0, 1, 2
 
-RUN = 6
+PSUM_BANKS = 8
+TRANSPOSE_BANKS = PSUM_BANKS - 2
+RUN = 4
 PAIR = 2
 VECTOR_EVERY = 6
 AHEAD = 3
@@ -69,7 +71,7 @@ def tile_custommodel_pb_t_kernel(tc, te, fe_n, loc_n, glob_n, logit_scale, logit
         stage = ctx.enter_context(tc.tile_pool(name="stage", bufs=2 * RUN // PAIR))
         packed = ctx.enter_context(tc.tile_pool(name="packed", bufs=3 * RUN // PAIR))
         sums = ctx.enter_context(tc.tile_pool(name="sums", bufs=2))
-        banks = ctx.enter_context(tc.psum_pool(name="banks", bufs=RUN))
+        banks = ctx.enter_context(tc.psum_pool(name="banks", bufs=TRANSPOSE_BANKS))
         products = ctx.enter_context(tc.psum_pool(name="products", bufs=1))
         ctx.enter_context(tc.manual_schedule())
 

@@ -38,7 +38,7 @@ PSUM_BANKS = 8
 TRANSPOSE_BANKS = PSUM_BANKS - 2
 RUN = 4
 PAIR = 2
-VECTOR_EVERY = 6
+VECTOR_EVERY = 4
 AHEAD = 3
 FOLD = 4
 OUT_ROWS = P // FOLD

from contextlib import ExitStack

import concourse.mybir as mybir
from concourse.masks import make_identity

F32 = mybir.dt.float32
BF16 = mybir.dt.bfloat16
U32 = mybir.dt.uint32
U8 = mybir.dt.uint8
FP8X4 = mybir.dt.float8_e4m3fn_x4
ALU = mybir.AluOpType
ACT = mybir.ActivationFunctionType
AXIS = mybir.AxisListType

P = 128
FRAMES = 4096
FEATURES = 1024
QUERIES = 128
CLIP = 8
MAIN_WEIGHT = 0.9
SIDE_WEIGHT = 0.05

FLOPS = 2 * 3 * QUERIES * FRAMES * FEATURES

TILES = FRAMES // P
CLIPS_PER_PARTITION = TILES // CLIP
K_PASS = 4 * P
PASSES = FEATURES // K_PASS
WORDS = FEATURES // 2
WORD_BLOCKS = WORDS // P
HALVES = WORD_BLOCKS // PASSES
BLOCK_TILES = 4
BLOCKS = TILES // BLOCK_TILES

FE, LOC, GLOB = 0, 1, 2

PSUM_BANKS = 8
TRANSPOSE_BANKS = PSUM_BANKS - 2
RUN = 4
PAIR = 2
VECTOR_EVERY = 4
AHEAD = 3
FOLD = 4
OUT_ROWS = P // FOLD


def work_list():
    tiles = []
    for block in range(BLOCKS):
        for j in range(BLOCK_TILES):
            tiles.append((LOC, block, j))
            tiles.append((GLOB, block, j))
        for j in range(BLOCK_TILES):
            tiles.append((FE, block, j))
    return tiles


def tile_custommodel_pb_t_kernel(tc, te, fe_n, loc_n, glob_n, logit_scale, logit_bias, out):
    nc = tc.nc
    streams = {
        FE: fe_n.rearrange("(p t) d -> p t d", t=TILES),
        LOC: loc_n.rearrange("(p t) d -> p t d", t=TILES),
        GLOB: glob_n.rearrange("(p t) d -> p t d", t=TILES),
    }
    tiles = work_list()
    rounds = [tiles[i : i + RUN] for i in range(0, len(tiles), RUN)]

    with ExitStack() as ctx:
        keep = ctx.enter_context(tc.tile_pool(name="keep", bufs=1))
        frames = ctx.enter_context(tc.tile_pool(name="frames", bufs=3 * AHEAD))
        stage = ctx.enter_context(tc.tile_pool(name="stage", bufs=2 * RUN // PAIR))
        packed = ctx.enter_context(tc.tile_pool(name="packed", bufs=3 * RUN // PAIR))
        sums = ctx.enter_context(tc.tile_pool(name="sums", bufs=2))
        banks = ctx.enter_context(tc.psum_pool(name="banks", bufs=TRANSPOSE_BANKS))
        products = ctx.enter_context(tc.psum_pool(name="products", bufs=1))
        ctx.enter_context(tc.manual_schedule())

        loaded = {}

        def load(stream, block, first, count):
            if first == 0:
                x = frames.tile([P, BLOCK_TILES, FEATURES], BF16, name="x")
                loaded[(stream, block)] = x
            t0 = block * BLOCK_TILES + first
            nc.sync.dma_start(
                out=loaded[(stream, block)][:, first : first + count, :],
                in_=streams[stream][:, t0 : t0 + count, :],
            )

        def transpose_words(rows):
            bank = banks.tile([P, WORD_BLOCKS, P], F32, name="bank")
            words = rows.bitcast(F32)
            for w in range(WORD_BLOCKS):
                nc.tensor.transpose(bank[:, w, :], words[:, w * P : (w + 1) * P], identity[:])
            return bank

        def regroup(copy, bank, grouped_rows):
            copy(
                out=grouped_rows.bitcast(F32).rearrange("p (g r u) -> p g r u", g=PASSES, u=HALVES),
                in_=bank[:].rearrange("p (g u) r -> p g r u", u=HALVES),
            )

        te_rows = keep.tile([P, FEATURES], BF16, name="te_rows")
        nc.sync.dma_start(out=te_rows[:], in_=te)
        scale_raw = keep.tile([P, 1], BF16, name="scale_raw")
        nc.scalar.dma_start(out=scale_raw[:], in_=logit_scale.partition_broadcast(P))
        bias_raw = keep.tile([P, 1], BF16, name="bias_raw")
        nc.scalar.dma_start(out=bias_raw[:], in_=logit_bias.partition_broadcast(P))

        for first in range(0, BLOCK_TILES, PAIR):
            load(LOC, 0, first, PAIR)
            load(GLOB, 0, first, PAIR)
        load(FE, 0, 0, BLOCK_TILES)
        for block in range(1, AHEAD):
            for stream in (LOC, GLOB, FE):
                load(stream, block, 0, BLOCK_TILES)

        identity = keep.tile([P, P], F32, name="identity")
        make_identity(nc, identity[:])

        gain = keep.tile([P, 1], F32, name="gain")
        nc.scalar.activation(out=gain[:], in_=scale_raw[:], func=ACT.Exp)

        owner = keep.tile([P, OUT_ROWS], F32, name="owner")
        nc.vector.tensor_reduce(
            out=owner[:], in_=identity[:].rearrange("p (m b) -> p m b", b=FOLD), axis=AXIS.X, op=ALU.add
        )
        gather = keep.tile([P, FOLD, OUT_ROWS], F32, name="gather")
        nc.vector.tensor_copy(out=gather[:], in_=owner[:].unsqueeze(1).to_broadcast([P, FOLD, OUT_ROWS]))
        place = keep.tile([P, FOLD], F32, name="place")
        nc.vector.tensor_reduce(
            out=place[:], in_=identity[:].rearrange("p (m b) -> p b m", b=FOLD), axis=AXIS.X, op=ALU.add
        )

        te_bank = transpose_words(te_rows[:])
        te_grouped = keep.tile([P, FEATURES], BF16, name="te_grouped", align_bytes=64)
        regroup(nc.vector.tensor_copy, te_bank, te_grouped[:])
        te_codes = keep.tile([P, PASSES * QUERIES], U32, name="te_codes", align_bytes=64)
        te_scales = keep.tile([P, PASSES * QUERIES], U8, name="te_scales", align_bytes=64)
        nc.vector.quantize_mx(out=te_codes[:].bitcast(FP8X4), scales=te_scales[:], in_=te_grouped[:])
        bias = keep.tile([P, 1], F32, name="bias")
        nc.vector.tensor_copy(out=bias[:], in_=bias_raw[:])
        main_gain = keep.tile([P, 1], F32, name="main_gain")
        nc.vector.tensor_scalar_mul(out=main_gain[:], in0=gain[:], scalar1=MAIN_WEIGHT)
        side_gain = keep.tile([P, 1], F32, name="side_gain")
        nc.vector.tensor_scalar_mul(out=side_gain[:], in0=gain[:], scalar1=SIDE_WEIGHT)

        logits = keep.tile([P, CLIPS_PER_PARTITION, CLIP], F32, name="logits")

        def transpose_round(step):
            filled = []
            for stream, block, j in rounds[step]:
                filled.append(transpose_words(loaded[(stream, block)][:, j, :]))
                if j == BLOCK_TILES - 1 and block + AHEAD < BLOCKS:
                    load(stream, block + AHEAD, 0, BLOCK_TILES)
            pairs = []
            for n, bank in enumerate(filled):
                if n % PAIR == 0:
                    grouped = stage.tile([P, PAIR * FEATURES], BF16, name="grouped", align_bytes=64)
                    pairs.append(grouped)
                copy = nc.vector.tensor_copy if (step * RUN + n) % VECTOR_EVERY == 0 else nc.scalar.copy
                s = n % PAIR
                regroup(copy, bank, pairs[-1][:, s * FEATURES : (s + 1) * FEATURES])
            return pairs

        def quantise_round(pairs):
            quantised = []
            for grouped in pairs:
                codes = packed.tile([P, PAIR * PASSES * P], U32, name="codes", align_bytes=64)
                scales = packed.tile([P, PAIR * PASSES * P], U8, name="scales", align_bytes=64)
                nc.vector.quantize_mx(out=codes[:].bitcast(FP8X4), scales=scales[:], in_=grouped[:])
                quantised.append((codes, scales))
            return quantised

        current = {}

        def multiply_round(step, quantised):
            for n, (stream, block, j) in enumerate(rounds[step]):
                codes, scales = quantised[n // PAIR]
                if j == 0 and stream == FE:
                    current["main"] = products.tile([P, BLOCK_TILES * QUERIES], F32, name="main")
                if j == 0 and stream == LOC:
                    current["side"] = products.tile([P, BLOCK_TILES * QUERIES], F32, name="side")
                product = current["main"] if stream == FE else current["side"]
                for g in range(PASSES):
                    cols = slice(((n % PAIR) * PASSES + g) * P, ((n % PAIR) * PASSES + g + 1) * P)
                    te_cols = slice(g * QUERIES, (g + 1) * QUERIES)
                    nc.tensor.matmul_mx(
                        out=product[:, j * QUERIES : (j + 1) * QUERIES],
                        lhsT=codes[:, cols].bitcast(FP8X4),
                        lhsT_scale=scales[:, cols],
                        rhs=te_codes[:, te_cols].bitcast(FP8X4),
                        rhs_scale=te_scales[:, te_cols],
                        start=(stream != GLOB and g == 0),
                        stop=(stream != LOC and g == PASSES - 1),
                    )
                if j == BLOCK_TILES - 1 and stream == GLOB:
                    current["weighted"] = sums.tile([P, BLOCK_TILES * QUERIES], F32, name="weighted")
                    nc.scalar.activation(
                        out=current["weighted"][:],
                        in_=product[:],
                        func=ACT.Identity,
                        scale=side_gain[:, 0:1],
                        bias=bias[:, 0:1],
                    )
                if j == BLOCK_TILES - 1 and stream == FE:
                    fused = sums.tile([P, BLOCK_TILES, QUERIES], F32, name="fused")
                    nc.vector.scalar_tensor_tensor(
                        out=fused[:].rearrange("p t q -> p (t q)"),
                        in0=product[:],
                        scalar=main_gain[:, 0:1],
                        in1=current["weighted"][:],
                        op0=ALU.mult,
                        op1=ALU.add,
                    )
                    nc.vector.tensor_reduce(
                        out=logits[:].rearrange("p c j -> p (c j)")[:, block * BLOCK_TILES : (block + 1) * BLOCK_TILES],
                        in_=fused[:],
                        axis=AXIS.X,
                        op=ALU.max,
                    )

        grouped_of = {}
        quantised_of = {}
        for step in range(len(rounds) + 2):
            if step < len(rounds):
                grouped_of[step] = transpose_round(step)
            if 1 <= step <= len(rounds):
                quantised_of[step - 1] = quantise_round(grouped_of[step - 1])
            if step >= 2:
                multiply_round(step - 2, quantised_of[step - 2])

        shape = [P, CLIPS_PER_PARTITION, CLIP]
        top = keep.tile([P, CLIPS_PER_PARTITION], F32, name="top")
        nc.vector.tensor_reduce(out=top[:], in_=logits[:], axis=AXIS.X, op=ALU.max)
        shifted = keep.tile(shape, F32, name="shifted")
        nc.vector.tensor_tensor(
            out=shifted[:], in0=logits[:], in1=top[:].unsqueeze(2).to_broadcast(shape), op=ALU.subtract
        )
        terms = keep.tile([P, 2] + shape[1:], F32, name="terms")
        nc.scalar.activation(out=terms[:, 0], in_=shifted[:], func=ACT.Exp)
        nc.vector.tensor_tensor(out=terms[:, 1], in0=terms[:, 0], in1=logits[:], op=ALU.mult)
        totals = keep.tile([P, 2 * CLIPS_PER_PARTITION], F32, name="totals")
        nc.vector.tensor_reduce(
            out=totals[:], in_=terms[:].rearrange("p h c j -> p (h c) j"), axis=AXIS.X, op=ALU.add
        )

        wide = [P, FOLD, 2 * CLIPS_PER_PARTITION]
        spread = keep.tile(wide, F32, name="spread")
        nc.vector.tensor_tensor(
            out=spread[:],
            in0=totals[:].unsqueeze(1).to_broadcast(wide),
            in1=place[:].unsqueeze(2).to_broadcast(wide),
            op=ALU.mult,
        )
        folded = banks.tile([P, FOLD, 2, CLIPS_PER_PARTITION], F32, name="folded", tag="bank")
        nc.tensor.matmul(
            out=folded[:].rearrange("p b h c -> p (b h c)"),
            lhsT=gather[:].rearrange("p r m -> p (r m)"),
            rhs=spread[:].rearrange("p b k -> p (b k)"),
            start=True,
            stop=True,
        )
        inverse = keep.tile([P, FOLD, CLIPS_PER_PARTITION], F32, name="inverse")
        nc.vector.reciprocal(out=inverse[:], in_=folded[:, :, 0, :])
        pooled = keep.tile([P, FOLD, CLIPS_PER_PARTITION], F32, name="pooled")
        nc.vector.tensor_tensor(out=pooled[:], in0=folded[:, :, 1, :], in1=inverse[:], op=ALU.mult)
        nc.sync.dma_start(
            out=out.rearrange("o (m k) -> (o m) k", k=FOLD * CLIPS_PER_PARTITION),
            in_=pooled[0:OUT_ROWS].rearrange("p b c -> p (b c)"),
        )
